import numpy as np
import ml_dtypes


def mxq(x, axis, fmt="e4m3"):
    dtype, down = {"e4m3": (ml_dtypes.float8_e4m3fn, 7), "e5m2": (ml_dtypes.float8_e5m2, 14)}[fmt]
    v = np.moveaxis(np.asarray(x, np.float32).astype(ml_dtypes.bfloat16).astype(np.float64), axis, -1)
    blocks = v.reshape(v.shape[:-1] + (-1, 32))
    amax = np.abs(blocks).max(-1, keepdims=True)
    byte = np.maximum(np.where(amax > 0, np.frexp(amax)[1] - 1 + 127, 0) - down, 1)
    scale = np.exp2(byte - 127.0)
    codes = (blocks / scale).astype(np.float32).astype(dtype).astype(np.float64)
    return np.moveaxis((codes * scale).reshape(v.shape), -1, axis)


WIDE = False


def mx_kscale(k):
    if not WIDE:
        return np.ones(k)
    levels = np.array([10, -10, 5, -5, 0])
    if k % 512:
        return np.exp2(np.random.permutation(np.resize(levels, k // 32))).repeat(32)
    a = np.empty((k // 512, 16))
    for p in range(k // 512):
        a[p, :8] = np.random.permutation(np.resize(levels, 8))
        for g in range(8):
            far = levels[np.abs(levels - a[p, g]) >= 10]
            a[p, g + 8] = far[np.random.randint(len(far))]
    return np.exp2(a.ravel()).repeat(32)


BF16 = ml_dtypes.bfloat16


def bf(x):
    return np.asarray(x, np.float32).astype(BF16)


def f64(x):
    return np.asarray(x).astype(np.float64)


T, B, D, H, HD, A = 2048, 2, 1024, 1, 128, 128
HH = H * HD
HA = H * A
N = HH + HH + HA + HA
EPS = 1e-5
QK = 1.5


def layer_norm(x, w, b):
    mu = x.mean(-1, keepdims=True)
    var = np.square(x - mu).mean(-1, keepdims=True)
    return (x - mu) * (1.0 / np.sqrt(var + EPS)) * w + b


def setup_inputs():
    s = mx_kscale(D)
    col = np.concatenate([np.ones(HH + HH), QK * np.ones(HA + HA)])
    return {"src": bf(np.random.standard_normal((T, B, D))),
            "ln1_w": bf((1.0 + 0.1 * np.random.standard_normal(D)) * s),
            "ln1_b": bf(0.1 * np.random.standard_normal(D) * s),
            "w_uvqk": bf(np.random.standard_normal((D, N)) * col / np.sqrt(D) / s[:, None]),
            "b_uvqk": bf(0.1 * np.random.standard_normal(N))}


def reference(src, ln1_w, ln1_b, w_uvqk, b_uvqk):
    src_norm = layer_norm(f64(src), f64(ln1_w), f64(ln1_b))
    return (mxq(src_norm, 2, "e4m3") @ mxq(f64(w_uvqk), 0, "e4m3")) + f64(b_uvqk)

@@ -1,0 +1,213 @@
+import concourse.mybir as mybir
+from concourse.masks import make_identity
+
+F32 = mybir.dt.float32
+BF16 = mybir.dt.bfloat16
+U32 = mybir.dt.uint32
+U8 = mybir.dt.uint8
+FP8X4 = mybir.dt.float8_e4m3fn_x4
+ALU = mybir.AluOpType
+ACT = mybir.ActivationFunctionType
+
+P = 128
+ROWS = 2048 * 2
+D = 1024
+N = 512
+EPS = 1e-5
+PACK = 4
+K_PASS = P * PACK
+PASSES = D // K_PASS
+CHUNKS = D // P
+BN_WIDTH = 512
+BN_PARTS = D // BN_WIDTH
+UNIT_TILES = 2
+UNIT_COLS = UNIT_TILES * P
+UNITS = ROWS // UNIT_COLS
+BANK_F32 = 512
+BANK_CHUNKS = BANK_F32 // UNIT_COLS
+PIPELINE_DEPTH = 4
+
+FLOPS = 2 * ROWS * D * N
+
+
+def side_by_side(copy, grouped, planes):
+    copy(
+        out=grouped.rearrange("p (c i) t -> p c t i", i=4),
+        in_=planes.rearrange("p t (c i) -> p c t i", i=4),
+    )
+
+
+def tile_stulayer_pa_t_kernel(tc, src, ln1_w, ln1_b, w_uvqk, b_uvqk, out):
+    nc = tc.nc
+    src_units = src.flatten_outer_dims().rearrange("(u p j) d -> u p j d", p=P, j=UNIT_TILES)
+    out_units = out.flatten_outer_dims().rearrange("(u p j) n -> u p j n", p=P, j=UNIT_TILES)
+
+    with (
+        tc.tile_pool(name="keep", bufs=1) as keep,
+        tc.tile_pool(name="stat", bufs=4) as stat,
+        tc.tile_pool(name="work", bufs=3) as work,
+        tc.psum_pool(name="turned", bufs=4) as turned_pool,
+        tc.psum_pool(name="sums", bufs=4) as sums_pool,
+        tc.manual_schedule(),
+    ):
+        x = []
+        for u in range(UNITS):
+            x.append(keep.tile([P, UNIT_TILES, D], BF16, name="x%d" % u))
+        w_planes = keep.tile([P, PASSES, PACK, N], BF16)
+        nc.sync.dma_start(out=x[0][:], in_=src_units[0])
+        nc.sync.dma_start(
+            out=w_planes[:], in_=w_uvqk.rearrange("(g p t) n -> p g t n", t=PACK, p=P)
+        )
+        bias = keep.tile([P, N], BF16)
+        for u in range(1, UNITS):
+            nc.sync.dma_start(out=x[u][:], in_=src_units[u])
+            if u == PIPELINE_DEPTH:
+                nc.sync.dma_start(out=bias[:], in_=b_uvqk.partition_broadcast(P))
+
+        gain_bf16 = keep.tile([P, PASSES, PACK], BF16)
+        shift_bf16 = keep.tile([P, PASSES, PACK], BF16)
+        nc.scalar.dma_start(out=gain_bf16[:], in_=ln1_w.rearrange("(g p t) -> p g t", t=PACK, p=P))
+        nc.scalar.dma_start(out=shift_bf16[:], in_=ln1_b.rearrange("(g p t) -> p g t", t=PACK, p=P))
+
+        ident = keep.tile([P, P], F32)
+        make_identity(nc, ident[:])
+        minus_half = keep.tile([P, UNIT_TILES], F32)
+        nc.vector.memset(minus_half[:], -0.5)
+
+        gain_shift = keep.tile([P, 2 * CHUNKS], F32)
+        nc.scalar.copy(
+            out=gain_shift[:, 0:CHUNKS], in_=gain_bf16[:].rearrange("p g t -> p (g t)")
+        )
+        nc.scalar.copy(
+            out=gain_shift[:, CHUNKS : 2 * CHUNKS], in_=shift_bf16[:].rearrange("p g t -> p (g t)")
+        )
+
+        w_grouped = keep.tile([P, PASSES, N, PACK], BF16, align_bytes=64)
+        w_codes = keep.tile([P, PASSES, N], U32, align_bytes=64)
+        w_scales = keep.tile([P, PASSES, N], U8, align_bytes=64)
+        for g in range(PASSES):
+            side_by_side(nc.scalar.copy, w_grouped[:, g], w_planes[:, g])
+
+        def quantise_weights():
+            nc.vector.quantize_mx(
+                out=w_codes[:].rearrange("p g n -> p (g n)").bitcast(FP8X4),
+                scales=w_scales[:].rearrange("p g n -> p (g n)"),
+                in_=w_grouped[:].rearrange("p g n t -> p (g n t)"),
+            )
+
+        mean_var = {}
+        normed = {}
+        grouped_of = {}
+        codes_of = {}
+        sums_of = {}
+
+        def statistics(u):
+            parts = stat.tile([P, UNIT_TILES, BN_PARTS, 6], F32)
+            mv = stat.tile([P, UNIT_TILES, 2], F32)
+            for j in range(UNIT_TILES):
+                for b in range(BN_PARTS):
+                    nc.vector.bn_stats(
+                        out=parts[:, j, b, :], in_=x[u][:, j, b * BN_WIDTH : (b + 1) * BN_WIDTH]
+                    )
+                nc.vector.bn_aggr(out=mv[:, j, :], in_=parts[:, j].rearrange("p b s -> p (b s)"))
+            mean_var[u] = mv
+
+        def normalise(u):
+            mv = mean_var[u]
+            var_eps = stat.tile([P, UNIT_TILES], F32)
+            rstd = stat.tile([P, UNIT_TILES], F32)
+            neg_mean = stat.tile([P, UNIT_TILES], F32)
+            nc.gpsimd.tensor_scalar(
+                out=var_eps[:], in0=mv[:, :, 1], scalar1=1.0, scalar2=EPS, op0=ALU.mult, op1=ALU.add
+            )
+            nc.gpsimd.tensor_tensor(out=rstd[:], in0=var_eps[:], in1=minus_half[:], op=ALU.pow)
+            nc.gpsimd.tensor_scalar(
+                out=neg_mean[:], in0=mv[:, :, 0], scalar1=-1.0, scalar2=0.0, op0=ALU.mult, op1=ALU.add
+            )
+            y = work.tile([P, UNIT_TILES, D], F32)
+            for j in range(UNIT_TILES):
+                nc.gpsimd.tensor_scalar(
+                    out=y[:, j, :].rearrange("p (g t q) -> p g t q", g=PASSES, t=PACK),
+                    in0=x[u][:, j, :].rearrange("p (g q t) -> p g t q", g=PASSES, t=PACK),
+                    scalar1=neg_mean[:, j : j + 1],
+                    scalar2=rstd[:, j : j + 1],
+                    op0=ALU.add,
+                    op1=ALU.mult,
+                )
+            normed[u] = y
+
+        def turn_and_scale(u):
+            y = normed[u]
+            planes = work.tile([P, CHUNKS, UNIT_COLS], BF16)
+            for first in range(0, CHUNKS, BANK_CHUNKS):
+                turned = turned_pool.tile([P, BANK_CHUNKS, UNIT_COLS], F32, tag="turned")
+                for b in range(BANK_CHUNKS):
+                    c = first + b
+                    for j in range(UNIT_TILES):
+                        nc.tensor.transpose(
+                            turned[:, b, j * P : (j + 1) * P], y[:, j, c * P : (c + 1) * P], ident[:]
+                        )
+                for b in range(BANK_CHUNKS):
+                    c = first + b
+                    nc.scalar.activation(
+                        out=planes[:, c, :],
+                        in_=turned[:, b, :],
+                        func=ACT.Identity,
+                        scale=gain_shift[:, c : c + 1],
+                        bias=gain_shift[:, CHUNKS + c : CHUNKS + c + 1],
+                    )
+            grouped = work.tile([P, PASSES, UNIT_COLS, PACK], BF16, align_bytes=64)
+            for g in range(PASSES):
+                side_by_side(nc.scalar.copy, grouped[:, g], planes[:, g * PACK : (g + 1) * PACK, :])
+            grouped_of[u] = grouped
+
+        def quantise(u):
+            codes = work.tile([P, PASSES, UNIT_COLS], U32, align_bytes=64)
+            scales = work.tile([P, PASSES, UNIT_COLS], U8, align_bytes=64)
+            nc.vector.quantize_mx(
+                out=codes[:].rearrange("p g c -> p (g c)").bitcast(FP8X4),
+                scales=scales[:].rearrange("p g c -> p (g c)"),
+                in_=grouped_of[u][:].rearrange("p g c t -> p (g c t)"),
+            )
+            codes_of[u] = (codes, scales)
+
+        def project(u):
+            codes, scales = codes_of[u]
+            sums_of[u] = []
+            for j in range(UNIT_TILES):
+                rows = slice(j * P, (j + 1) * P)
+                sums = sums_pool.tile([P, N], F32)
+                for g in range(PASSES):
+                    nc.tensor.matmul_mx(
+                        out=sums[:],
+                        lhsT=codes[:, g, rows].bitcast(FP8X4),
+                        lhsT_scale=scales[:, g, rows],
+                        rhs=w_codes[:, g, :].bitcast(FP8X4),
+                        rhs_scale=w_scales[:, g, :],
+                        start=(g == 0),
+                        stop=(g == PASSES - 1),
+                    )
+                sums_of[u].append(sums)
+
+        def finish(u):
+            result = work.tile([P, UNIT_TILES, N], F32)
+            for j in range(UNIT_TILES):
+                nc.vector.tensor_tensor(
+                    out=result[:, j, :], in0=sums_of[u][j][:], in1=bias[:], op=ALU.add
+                )
+            nc.sync.dma_start(out=out_units[u], in_=result[:])
+
+        for step in range(UNITS + PIPELINE_DEPTH):
+            if step < UNITS:
+                statistics(step)
+            if step == 2:
+                quantise_weights()
+            if 0 <= step - 1 < UNITS:
+                normalise(step - 1)
+            if 0 <= step - 2 < UNITS:
+                turn_and_scale(step - 2)
+            if 0 <= step - 3 < UNITS:
+                quantise(step - 3)
+                project(step - 3)
+            if 0 <= step - PIPELINE_DEPTH < UNITS:
+                finish(step - PIPELINE_DEPTH)

@@ -20,12 +20,18 @@ PASSES = D // K_PASS
 CHUNKS = D // P
 BN_WIDTH = 512
 BN_PARTS = D // BN_WIDTH
-UNIT_TILES = 2
-UNIT_COLS = UNIT_TILES * P
-UNITS = ROWS // UNIT_COLS
 BANK_F32 = 512
-BANK_CHUNKS = BANK_F32 // UNIT_COLS
-PIPELINE_DEPTH = 4
+WIDTHS = [1, 1] + [2] * 14 + [1, 1]
+UNITS = len(WIDTHS)
+WIDEST = max(WIDTHS)
+FIRST_TILE = [sum(WIDTHS[:u]) for u in range(UNITS)]
+LAST_TILE = [FIRST_TILE[u] + WIDTHS[u] - 1 for u in range(UNITS)]
+PLACE = [(u, j) for u in range(UNITS) for j in range(WIDTHS[u])]
+
+TURN_LAG = 4
+QUANTISE_LAG = 4
+PROJECT_LAG = 1
+FINISH_LAG = 1
 
 FLOPS = 2 * ROWS * D * N
 
@@ -39,8 +45,13 @@ def side_by_side(copy, grouped, planes):
 
 def tile_stulayer_pa_t_kernel(tc, src, ln1_w, ln1_b, w_uvqk, b_uvqk, out):
     nc = tc.nc
-    src_units = src.flatten_outer_dims().rearrange("(u p j) d -> u p j d", p=P, j=UNIT_TILES)
-    out_units = out.flatten_outer_dims().rearrange("(u p j) n -> u p j n", p=P, j=UNIT_TILES)
+    src_rows = src.flatten_outer_dims()
+    out_rows = out.flatten_outer_dims()
+
+    def rows_of(tensor, u):
+        n = WIDTHS[u]
+        first = FIRST_TILE[u] * P
+        return tensor[first : first + n * P, :].rearrange("(p j) d -> p j d", j=n)
 
     with (
         tc.tile_pool(name="keep", bufs=1) as keep,
@@ -52,16 +63,16 @@ def tile_stulayer_pa_t_kernel(tc, src, ln1_w, ln1_b, w_uvqk, b_uvqk, out):
     ):
         x = []
         for u in range(UNITS):
-            x.append(keep.tile([P, UNIT_TILES, D], BF16, name="x%d" % u))
+            x.append(keep.tile([P, WIDTHS[u], D], BF16, name="x%d" % u))
         w_planes = keep.tile([P, PASSES, PACK, N], BF16)
-        nc.sync.dma_start(out=x[0][:], in_=src_units[0])
-        nc.sync.dma_start(
-            out=w_planes[:], in_=w_uvqk.rearrange("(g p t) n -> p g t n", t=PACK, p=P)
-        )
         bias = keep.tile([P, N], BF16)
-        for u in range(1, UNITS):
-            nc.sync.dma_start(out=x[u][:], in_=src_units[u])
-            if u == PIPELINE_DEPTH:
+        for u in range(UNITS):
+            nc.sync.dma_start(out=x[u][:], in_=rows_of(src_rows, u))
+            if u == 1:
+                nc.sync.dma_start(
+                    out=w_planes[:], in_=w_uvqk.rearrange("(g p t) n -> p g t n", t=PACK, p=P)
+                )
+            if u == 5:
                 nc.sync.dma_start(out=bias[:], in_=b_uvqk.partition_broadcast(P))
 
         gain_bf16 = keep.tile([P, PASSES, PACK], BF16)
@@ -71,13 +82,10 @@ def tile_stulayer_pa_t_kernel(tc, src, ln1_w, ln1_b, w_uvqk, b_uvqk, out):
 
         ident = keep.tile([P, P], F32)
         make_identity(nc, ident[:])
-        minus_half = keep.tile([P, UNIT_TILES], F32)
+        minus_half = keep.tile([P, WIDEST], F32)
         nc.vector.memset(minus_half[:], -0.5)
-
         gain_shift = keep.tile([P, 2 * CHUNKS], F32)
-        nc.scalar.copy(
-            out=gain_shift[:, 0:CHUNKS], in_=gain_bf16[:].rearrange("p g t -> p (g t)")
-        )
+        nc.scalar.copy(out=gain_shift[:, 0:CHUNKS], in_=gain_bf16[:].rearrange("p g t -> p (g t)"))
         nc.scalar.copy(
             out=gain_shift[:, CHUNKS : 2 * CHUNKS], in_=shift_bf16[:].rearrange("p g t -> p (g t)")
         )
@@ -95,37 +103,49 @@ def tile_stulayer_pa_t_kernel(tc, src, ln1_w, ln1_b, w_uvqk, b_uvqk, out):
                 in_=w_grouped[:].rearrange("p g n t -> p (g n t)"),
             )
 
+        parts_of = {}
         mean_var = {}
         normed = {}
+        turned_of = {}
+        planes_of = {}
         grouped_of = {}
         codes_of = {}
         sums_of = {}
+        result_of = {}
 
-        def statistics(u):
-            parts = stat.tile([P, UNIT_TILES, BN_PARTS, 6], F32)
-            mv = stat.tile([P, UNIT_TILES, 2], F32)
-            for j in range(UNIT_TILES):
-                for b in range(BN_PARTS):
-                    nc.vector.bn_stats(
-                        out=parts[:, j, b, :], in_=x[u][:, j, b * BN_WIDTH : (b + 1) * BN_WIDTH]
-                    )
-                nc.vector.bn_aggr(out=mv[:, j, :], in_=parts[:, j].rearrange("p b s -> p (b s)"))
-            mean_var[u] = mv
+        def statistics(tile):
+            u, j = PLACE[tile]
+            if j == 0:
+                mean_var[u] = stat.tile([P, WIDTHS[u], 2], F32, name="mv")
+            parts_of[tile] = stat.tile([P, BN_PARTS, 6], F32, name="parts")
+            for b in range(BN_PARTS):
+                nc.vector.bn_stats(
+                    out=parts_of[tile][:, b, :], in_=x[u][:, j, b * BN_WIDTH : (b + 1) * BN_WIDTH]
+                )
+
+        def aggregate(tile):
+            u, j = PLACE[tile]
+            nc.vector.bn_aggr(
+                out=mean_var[u][:, j, :], in_=parts_of[tile][:].rearrange("p b s -> p (b s)")
+            )
 
         def normalise(u):
+            n = WIDTHS[u]
             mv = mean_var[u]
-            var_eps = stat.tile([P, UNIT_TILES], F32)
-            rstd = stat.tile([P, UNIT_TILES], F32)
-            neg_mean = stat.tile([P, UNIT_TILES], F32)
+            var_eps = stat.tile([P, n], F32)
+            rstd = stat.tile([P, n], F32)
             nc.gpsimd.tensor_scalar(
                 out=var_eps[:], in0=mv[:, :, 1], scalar1=1.0, scalar2=EPS, op0=ALU.mult, op1=ALU.add
             )
-            nc.gpsimd.tensor_tensor(out=rstd[:], in0=var_eps[:], in1=minus_half[:], op=ALU.pow)
+            nc.gpsimd.tensor_tensor(
+                out=rstd[:], in0=var_eps[:], in1=minus_half[:, 0:n], op=ALU.pow
+            )
+            neg_mean = stat.tile([P, n], F32)
             nc.gpsimd.tensor_scalar(
                 out=neg_mean[:], in0=mv[:, :, 0], scalar1=-1.0, scalar2=0.0, op0=ALU.mult, op1=ALU.add
             )
-            y = work.tile([P, UNIT_TILES, D], F32)
-            for j in range(UNIT_TILES):
+            y = work.tile([P, n, D], F32)
+            for j in range(n):
                 nc.gpsimd.tensor_scalar(
                     out=y[:, j, :].rearrange("p (g t q) -> p g t q", g=PASSES, t=PACK),
                     in0=x[u][:, j, :].rearrange("p (g q t) -> p g t q", g=PASSES, t=PACK),
@@ -136,34 +156,54 @@ def tile_stulayer_pa_t_kernel(tc, src, ln1_w, ln1_b, w_uvqk, b_uvqk, out):
                 )
             normed[u] = y
 
-        def turn_and_scale(u):
+        def turn(u, g):
+            n = WIDTHS[u]
             y = normed[u]
-            planes = work.tile([P, CHUNKS, UNIT_COLS], BF16)
-            for first in range(0, CHUNKS, BANK_CHUNKS):
-                turned = turned_pool.tile([P, BANK_CHUNKS, UNIT_COLS], F32, tag="turned")
-                for b in range(BANK_CHUNKS):
+            if g == 0:
+                turned_of[u] = []
+                planes_of[u] = work.tile([P, CHUNKS, n * P], BF16, name="planes")
+                grouped_of[u] = work.tile(
+                    [P, PASSES, n * P, PACK], BF16, align_bytes=64, name="grouped"
+                )
+            per_bank = BANK_F32 // (n * P)
+            for first in range(g * PACK, (g + 1) * PACK, per_bank):
+                turned = turned_pool.tile([P, per_bank, n * P], F32, tag="turned", name="turned")
+                for b in range(per_bank):
                     c = first + b
-                    for j in range(UNIT_TILES):
+                    for j in range(n):
                         nc.tensor.transpose(
                             turned[:, b, j * P : (j + 1) * P], y[:, j, c * P : (c + 1) * P], ident[:]
                         )
-                for b in range(BANK_CHUNKS):
-                    c = first + b
-                    nc.scalar.activation(
-                        out=planes[:, c, :],
-                        in_=turned[:, b, :],
-                        func=ACT.Identity,
-                        scale=gain_shift[:, c : c + 1],
-                        bias=gain_shift[:, CHUNKS + c : CHUNKS + c + 1],
-                    )
-            grouped = work.tile([P, PASSES, UNIT_COLS, PACK], BF16, align_bytes=64)
-            for g in range(PASSES):
-                side_by_side(nc.scalar.copy, grouped[:, g], planes[:, g * PACK : (g + 1) * PACK, :])
-            grouped_of[u] = grouped
+                turned_of[u].append(turned)
+
+        def scale(u, banks, on_vector):
+            n = WIDTHS[u]
+            per_bank = BANK_F32 // (n * P)
+            for bank in banks:
+                for b in range(per_bank):
+                    c = bank * per_bank + b
+                    gain = gain_shift[:, c : c + 1]
+                    shift = gain_shift[:, CHUNKS + c : CHUNKS + c + 1]
+                    into = planes_of[u][:, c, :]
+                    chunk = turned_of[u][bank][:, b, :]
+                    if on_vector:
+                        nc.vector.tensor_scalar(
+                            out=into, in0=chunk, scalar1=gain, scalar2=shift, op0=ALU.mult, op1=ALU.add
+                        )
+                    else:
+                        nc.scalar.activation(
+                            out=into, in_=chunk, func=ACT.Identity, scale=gain, bias=shift
+                        )
+
+        def group(u, g):
+            side_by_side(
+                nc.scalar.copy, grouped_of[u][:, g], planes_of[u][:, g * PACK : (g + 1) * PACK, :]
+            )
 
         def quantise(u):
-            codes = work.tile([P, PASSES, UNIT_COLS], U32, align_bytes=64)
-            scales = work.tile([P, PASSES, UNIT_COLS], U8, align_bytes=64)
+            n = WIDTHS[u]
+            codes = work.tile([P, PASSES, n * P], U32, align_bytes=64)
+            scales = work.tile([P, PASSES, n * P], U8, align_bytes=64)
             nc.vector.quantize_mx(
                 out=codes[:].rearrange("p g c -> p (g c)").bitcast(FP8X4),
                 scales=scales[:].rearrange("p g c -> p (g c)"),
@@ -171,43 +211,71 @@ def tile_stulayer_pa_t_kernel(tc, src, ln1_w, ln1_b, w_uvqk, b_uvqk, out):
             )
             codes_of[u] = (codes, scales)
 
-        def project(u):
+        def project(tile):
+            u, j = PLACE[tile]
             codes, scales = codes_of[u]
-            sums_of[u] = []
-            for j in range(UNIT_TILES):
-                rows = slice(j * P, (j + 1) * P)
-                sums = sums_pool.tile([P, N], F32)
-                for g in range(PASSES):
-                    nc.tensor.matmul_mx(
-                        out=sums[:],
-                        lhsT=codes[:, g, rows].bitcast(FP8X4),
-                        lhsT_scale=scales[:, g, rows],
-                        rhs=w_codes[:, g, :].bitcast(FP8X4),
-                        rhs_scale=w_scales[:, g, :],
-                        start=(g == 0),
-                        stop=(g == PASSES - 1),
-                    )
-                sums_of[u].append(sums)
-
-        def finish(u):
-            result = work.tile([P, UNIT_TILES, N], F32)
-            for j in range(UNIT_TILES):
-                nc.vector.tensor_tensor(
-                    out=result[:, j, :], in0=sums_of[u][j][:], in1=bias[:], op=ALU.add
+            rows = slice(j * P, (j + 1) * P)
+            sums_of[tile] = sums_pool.tile([P, N], F32, name="sums")
+            for g in range(PASSES):
+                nc.tensor.matmul_mx(
+                    out=sums_of[tile][:],
+                    lhsT=codes[:, g, rows].bitcast(FP8X4),
+                    lhsT_scale=scales[:, g, rows],
+                    rhs=w_codes[:, g, :].bitcast(FP8X4),
+                    rhs_scale=w_scales[:, g, :],
+                    start=(g == 0),
+                    stop=(g == PASSES - 1),
                 )
-            nc.sync.dma_start(out=out_units[u], in_=result[:])
 
-        for step in range(UNITS + PIPELINE_DEPTH):
-            if step < UNITS:
-                statistics(step)
-            if step == 2:
-                quantise_weights()
-            if 0 <= step - 1 < UNITS:
-                normalise(step - 1)
-            if 0 <= step - 2 < UNITS:
-                turn_and_scale(step - 2)
-            if 0 <= step - 3 < UNITS:
-                quantise(step - 3)
-                project(step - 3)
-            if 0 <= step - PIPELINE_DEPTH < UNITS:
-                finish(step - PIPELINE_DEPTH)
+        def finish(tile):
+            u, j = PLACE[tile]
+            n = WIDTHS[u]
+            if j == 0:
+                result_of[u] = work.tile([P, n, N], F32, name="result")
+            nc.vector.tensor_tensor(
+                out=result_of[u][:, j, :], in0=sums_of[tile][:], in1=bias[:], op=ALU.add
+            )
+            if j == n - 1:
+                nc.sync.dma_start(out=rows_of(out_rows, u), in_=result_of[u][:])
+
+        def vector_banks(u):
+            return [3] if WIDTHS[u] == WIDEST and u % 2 == 0 else []
+
+        def scale_on_scalar(u, g):
+            banks = len(turned_of[u]) // (g + 1)
+            mine = [b for b in range(g * banks, (g + 1) * banks) if b not in vector_banks(u)]
+            scale(u, mine, False)
+
+        def turn_and_scale(u):
+            for g in range(PASSES):
+                turn(u, g)
+                scale_on_scalar(u, g)
+                if g == 1:
+                    group(u, 0)
+                elif u > 0:
+                    group(u - 1, 1)
+            if u == UNITS - 1:
+                group(u, 1)
+
+        agenda = {}
+
+        def at(tick, rank, stage, *args):
+            agenda.setdefault(tick, []).append((rank, len(agenda[tick]) if tick in agenda else 0, stage, args))
+
+        for tile in range(FIRST_TILE[-1] + WIDTHS[-1]):
+            at(tile, 0, statistics, tile)
+            at(tile + 1, 1, aggregate, tile)
+        at(5, 2, quantise_weights)
+        for u in range(UNITS):
+            at(LAST_TILE[u] + 1, 4, normalise, u)
+            turning = LAST_TILE[u] + TURN_LAG
+            at(turning, 6, turn_and_scale, u)
+            at(turning, 7, scale, u, vector_banks(u), True)
+            at(turning + QUANTISE_LAG, 3, quantise, u)
+            for j in range(WIDTHS[u]):
+                projecting = turning + QUANTISE_LAG + PROJECT_LAG + j
+                at(projecting, 8, project, FIRST_TILE[u] + j)
+                at(projecting + FINISH_LAG, 5, finish, FIRST_TILE[u] + j)
+        for tick in sorted(agenda):
+            for rank, order, stage, args in sorted(agenda[tick], key=lambda entry: entry[:2]):
+                stage(*args)

@@ -238,13 +238,9 @@ def tile_stulayer_pa_t_kernel(tc, src, ln1_w, ln1_b, w_uvqk, b_uvqk, out):
             if j == n - 1:
                 nc.sync.dma_start(out=rows_of(out_rows, u), in_=result_of[u][:])
 
-        def vector_banks(u):
-            return [3] if WIDTHS[u] == WIDEST and u % 2 == 0 else []
-
         def scale_on_scalar(u, g):
             banks = len(turned_of[u]) // (g + 1)
-            mine = [b for b in range(g * banks, (g + 1) * banks) if b not in vector_banks(u)]
-            scale(u, mine, False)
+            scale(u, range(g * banks, (g + 1) * banks), False)
 
         def turn_and_scale(u):
             for g in range(PASSES):
@@ -270,7 +266,6 @@ def tile_stulayer_pa_t_kernel(tc, src, ln1_w, ln1_b, w_uvqk, b_uvqk, out):
             at(LAST_TILE[u] + 1, 4, normalise, u)
             turning = LAST_TILE[u] + TURN_LAG
             at(turning, 6, turn_and_scale, u)
-            at(turning, 7, scale, u, vector_banks(u), True)
             at(turning + QUANTISE_LAG, 3, quantise, u)
             for j in range(WIDTHS[u]):
                 projecting = turning + QUANTISE_LAG + PROJECT_LAG + j

@@ -25,13 +25,8 @@ WIDTHS = [1, 1] + [2] * 14 + [1, 1]
 UNITS = len(WIDTHS)
 WIDEST = max(WIDTHS)
 FIRST_TILE = [sum(WIDTHS[:u]) for u in range(UNITS)]
-LAST_TILE = [FIRST_TILE[u] + WIDTHS[u] - 1 for u in range(UNITS)]
-PLACE = [(u, j) for u in range(UNITS) for j in range(WIDTHS[u])]
-
-TURN_LAG = 4
-QUANTISE_LAG = 4
-PROJECT_LAG = 1
-FINISH_LAG = 1
+DEPTH = 5
+VECTOR_CHUNK = CHUNKS - 1
 
 FLOPS = 2 * ROWS * D * N
 
@@ -58,7 +53,8 @@ def tile_stulayer_pa_t_kernel(tc, src, ln1_w, ln1_b, w_uvqk, b_uvqk, out):
         tc.tile_pool(name="stat", bufs=4) as stat,
         tc.tile_pool(name="work", bufs=3) as work,
         tc.psum_pool(name="turned", bufs=4) as turned_pool,
-        tc.psum_pool(name="sums", bufs=4) as sums_pool,
+        tc.psum_pool(name="vector", bufs=1) as vector_pool,
+        tc.psum_pool(name="sums", bufs=3) as sums_pool,
         tc.manual_schedule(),
     ):
         x = []
@@ -103,7 +99,6 @@ def tile_stulayer_pa_t_kernel(tc, src, ln1_w, ln1_b, w_uvqk, b_uvqk, out):
                 in_=w_grouped[:].rearrange("p g n t -> p (g n t)"),
             )
 
-        parts_of = {}
         mean_var = {}
         normed = {}
         turned_of = {}
@@ -111,23 +106,20 @@ def tile_stulayer_pa_t_kernel(tc, src, ln1_w, ln1_b, w_uvqk, b_uvqk, out):
         grouped_of = {}
         codes_of = {}
         sums_of = {}
-        result_of = {}
 
-        def statistics(tile):
-            u, j = PLACE[tile]
-            if j == 0:
-                mean_var[u] = stat.tile([P, WIDTHS[u], 2], F32, name="mv")
-            parts_of[tile] = stat.tile([P, BN_PARTS, 6], F32, name="parts")
-            for b in range(BN_PARTS):
-                nc.vector.bn_stats(
-                    out=parts_of[tile][:, b, :], in_=x[u][:, j, b * BN_WIDTH : (b + 1) * BN_WIDTH]
+        def statistics(u):
+            n = WIDTHS[u]
+            parts = stat.tile([P, n, BN_PARTS, 6], F32, name="parts")
+            mean_var[u] = stat.tile([P, n, 2], F32, name="mv")
+            for j in range(n):
+                for b in range(BN_PARTS):
+                    nc.vector.bn_stats(
+                        out=parts[:, j, b, :], in_=x[u][:, j, b * BN_WIDTH : (b + 1) * BN_WIDTH]
+                    )
+            for j in range(n):
+                nc.vector.bn_aggr(
+                    out=mean_var[u][:, j, :], in_=parts[:, j].rearrange("p b s -> p (b s)")
                 )
-
-        def aggregate(tile):
-            u, j = PLACE[tile]
-            nc.vector.bn_aggr(
-                out=mean_var[u][:, j, :], in_=parts_of[tile][:].rearrange("p b s -> p (b s)")
-            )
 
         def normalise(u):
             n = WIDTHS[u]
@@ -160,40 +152,42 @@ def tile_stulayer_pa_t_kernel(tc, src, ln1_w, ln1_b, w_uvqk, b_uvqk, out):
             n = WIDTHS[u]
             y = normed[u]
             if g == 0:
-                turned_of[u] = []
                 planes_of[u] = work.tile([P, CHUNKS, n * P], BF16, name="planes")
                 grouped_of[u] = work.tile(
                     [P, PASSES, n * P, PACK], BF16, align_bytes=64, name="grouped"
                 )
             per_bank = BANK_F32 // (n * P)
-            for first in range(g * PACK, (g + 1) * PACK, per_bank):
-                turned = turned_pool.tile([P, per_bank, n * P], F32, tag="turned", name="turned")
-                for b in range(per_bank):
-                    c = first + b
-                    for j in range(n):
-                        nc.tensor.transpose(
-                            turned[:, b, j * P : (j + 1) * P], y[:, j, c * P : (c + 1) * P], ident[:]
-                        )
-                turned_of[u].append(turned)
+            for c in chunks_of(g):
+                if c == VECTOR_CHUNK:
+                    bank, slot = vector_pool.tile([P, per_bank, n * P], F32, name="for_vector"), 0
+                else:
+                    slot = c % per_bank
+                    if slot == 0:
+                        shared = turned_pool.tile([P, per_bank, n * P], F32, name="turned")
+                    bank = shared
+                turned_of[u, c] = bank[:, slot, :]
+                for j in range(n):
+                    nc.tensor.transpose(
+                        bank[:, slot, j * P : (j + 1) * P], y[:, j, c * P : (c + 1) * P], ident[:]
+                    )
 
-        def scale(u, banks, on_vector):
-            n = WIDTHS[u]
-            per_bank = BANK_F32 // (n * P)
-            for bank in banks:
-                for b in range(per_bank):
-                    c = bank * per_bank + b
-                    gain = gain_shift[:, c : c + 1]
-                    shift = gain_shift[:, CHUNKS + c : CHUNKS + c + 1]
-                    into = planes_of[u][:, c, :]
-                    chunk = turned_of[u][bank][:, b, :]
-                    if on_vector:
-                        nc.vector.tensor_scalar(
-                            out=into, in0=chunk, scalar1=gain, scalar2=shift, op0=ALU.mult, op1=ALU.add
-                        )
-                    else:
-                        nc.scalar.activation(
-                            out=into, in_=chunk, func=ACT.Identity, scale=gain, bias=shift
-                        )
+        def chunks_of(g):
+            return range(g * PACK, (g + 1) * PACK)
+
+        def scale(u, chunks, on_vector):
+            for c in chunks:
+                gain = gain_shift[:, c : c + 1]
+                shift = gain_shift[:, CHUNKS + c : CHUNKS + c + 1]
+                into = planes_of[u][:, c, :]
+                chunk = turned_of[u, c]
+                if on_vector:
+                    nc.vector.tensor_scalar(
+                        out=into, in0=chunk, scalar1=gain, scalar2=shift, op0=ALU.mult, op1=ALU.add
+                    )
+                else:
+                    nc.scalar.activation(
+                        out=into, in_=chunk, func=ACT.Identity, scale=gain, bias=shift
+                    )
 
         def group(u, g):
             side_by_side(
@@ -211,66 +205,60 @@ def tile_stulayer_pa_t_kernel(tc, src, ln1_w, ln1_b, w_uvqk, b_uvqk, out):
             )
             codes_of[u] = (codes, scales)
 
-        def project(tile):
-            u, j = PLACE[tile]
+        def project(u):
             codes, scales = codes_of[u]
-            rows = slice(j * P, (j + 1) * P)
-            sums_of[tile] = sums_pool.tile([P, N], F32, name="sums")
-            for g in range(PASSES):
-                nc.tensor.matmul_mx(
-                    out=sums_of[tile][:],
-                    lhsT=codes[:, g, rows].bitcast(FP8X4),
-                    lhsT_scale=scales[:, g, rows],
-                    rhs=w_codes[:, g, :].bitcast(FP8X4),
-                    rhs_scale=w_scales[:, g, :],
-                    start=(g == 0),
-                    stop=(g == PASSES - 1),
-                )
+            sums_of[u] = []
+            for j in range(WIDTHS[u]):
+                rows = slice(j * P, (j + 1) * P)
+                sums = sums_pool.tile([P, N], F32)
+                for g in range(PASSES):
+                    nc.tensor.matmul_mx(
+                        out=sums[:],
+                        lhsT=codes[:, g, rows].bitcast(FP8X4),
+                        lhsT_scale=scales[:, g, rows],
+                        rhs=w_codes[:, g, :].bitcast(FP8X4),
+                        rhs_scale=w_scales[:, g, :],
+                        start=(g == 0),
+                        stop=(g == PASSES - 1),
+                    )
+                sums_of[u].append(sums)
 
-        def finish(tile):
-            u, j = PLACE[tile]
+        def finish(u):
             n = WIDTHS[u]
-            if j == 0:
-                result_of[u] = work.tile([P, n, N], F32, name="result")
-            nc.vector.tensor_tensor(
-                out=result_of[u][:, j, :], in0=sums_of[tile][:], in1=bias[:], op=ALU.add
-            )
-            if j == n - 1:
-                nc.sync.dma_start(out=rows_of(out_rows, u), in_=result_of[u][:])
+            result = work.tile([P, n, N], F32)
+            for j in range(n):
+                nc.vector.tensor_tensor(
+                    out=result[:, j, :], in0=sums_of[u][j][:], in1=bias[:], op=ALU.add
+                )
+            nc.sync.dma_start(out=rows_of(out_rows, u), in_=result[:])
 
-        def scale_on_scalar(u, g):
-            banks = len(turned_of[u]) // (g + 1)
-            scale(u, range(g * banks, (g + 1) * banks), False)
+        def live(u):
+            return 0 <= u < UNITS
 
         def turn_and_scale(u):
             for g in range(PASSES):
                 turn(u, g)
-                scale_on_scalar(u, g)
-                if g == 1:
-                    group(u, 0)
-                elif u > 0:
+                scale(u, [c for c in chunks_of(g) if c != VECTOR_CHUNK], False)
+                if g == 0 and u > 0:
                     group(u - 1, 1)
-            if u == UNITS - 1:
-                group(u, 1)
+            group(u, 0)
 
-        agenda = {}
-
-        def at(tick, rank, stage, *args):
-            agenda.setdefault(tick, []).append((rank, len(agenda[tick]) if tick in agenda else 0, stage, args))
-
-        for tile in range(FIRST_TILE[-1] + WIDTHS[-1]):
-            at(tile, 0, statistics, tile)
-            at(tile + 1, 1, aggregate, tile)
-        at(5, 2, quantise_weights)
-        for u in range(UNITS):
-            at(LAST_TILE[u] + 1, 4, normalise, u)
-            turning = LAST_TILE[u] + TURN_LAG
-            at(turning, 6, turn_and_scale, u)
-            at(turning + QUANTISE_LAG, 3, quantise, u)
-            for j in range(WIDTHS[u]):
-                projecting = turning + QUANTISE_LAG + PROJECT_LAG + j
-                at(projecting, 8, project, FIRST_TILE[u] + j)
-                at(projecting + FINISH_LAG, 5, finish, FIRST_TILE[u] + j)
-        for tick in sorted(agenda):
-            for rank, order, stage, args in sorted(agenda[tick], key=lambda entry: entry[:2]):
-                stage(*args)
+        for step in range(UNITS + DEPTH):
+            fresh, ready, turning, turned, quantising, leaving = (step - d for d in range(DEPTH + 1))
+            if live(turned):
+                scale(turned, [VECTOR_CHUNK], True)
+            if live(fresh):
+                statistics(fresh)
+            if step == 3:
+                quantise_weights()
+            if live(ready):
+                normalise(ready)
+            if live(turning):
+                turn_and_scale(turning)
+            elif turned == UNITS - 1:
+                group(turned, 1)
+            if live(quantising):
+                quantise(quantising)
+                project(quantising)
+            if live(leaving):
+                finish(leaving)

@@ -100,6 +100,8 @@ def tile_stulayer_pa_t_kernel(tc, src, ln1_w, ln1_b, w_uvqk, b_uvqk, out):
             )
 
         mean_var = {}
+        var_eps = {}
+        neg_mean = {}
         normed = {}
         turned_of = {}
         planes_of = {}
@@ -121,27 +123,29 @@ def tile_stulayer_pa_t_kernel(tc, src, ln1_w, ln1_b, w_uvqk, b_uvqk, out):
                     out=mean_var[u][:, j, :], in_=parts[:, j].rearrange("p b s -> p (b s)")
                 )
 
+        def prepare(u):
+            n = WIDTHS[u]
+            var_eps[u] = stat.tile([P, n], F32, name="var_eps")
+            nc.vector.tensor_scalar(
+                out=var_eps[u][:], in0=mean_var[u][:, :, 1], scalar1=EPS, scalar2=None, op0=ALU.add
+            )
+            neg_mean[u] = stat.tile([P, n], F32, name="neg_mean")
+            nc.vector.tensor_scalar(
+                out=neg_mean[u][:], in0=mean_var[u][:, :, 0], scalar1=-1.0, scalar2=None, op0=ALU.mult
+            )
+
         def normalise(u):
             n = WIDTHS[u]
-            mv = mean_var[u]
-            var_eps = stat.tile([P, n], F32)
             rstd = stat.tile([P, n], F32)
-            nc.gpsimd.tensor_scalar(
-                out=var_eps[:], in0=mv[:, :, 1], scalar1=1.0, scalar2=EPS, op0=ALU.mult, op1=ALU.add
-            )
             nc.gpsimd.tensor_tensor(
-                out=rstd[:], in0=var_eps[:], in1=minus_half[:, 0:n], op=ALU.pow
-            )
-            neg_mean = stat.tile([P, n], F32)
-            nc.gpsimd.tensor_scalar(
-                out=neg_mean[:], in0=mv[:, :, 0], scalar1=-1.0, scalar2=0.0, op0=ALU.mult, op1=ALU.add
+                out=rstd[:], in0=var_eps[u][:], in1=minus_half[:, 0:n], op=ALU.pow
             )
             y = work.tile([P, n, D], F32)
             for j in range(n):
                 nc.gpsimd.tensor_scalar(
                     out=y[:, j, :].rearrange("p (g t q) -> p g t q", g=PASSES, t=PACK),
                     in0=x[u][:, j, :].rearrange("p (g q t) -> p g t q", g=PASSES, t=PACK),
-                    scalar1=neg_mean[:, j : j + 1],
+                    scalar1=neg_mean[u][:, j : j + 1],
                     scalar2=rstd[:, j : j + 1],
                     op0=ALU.add,
                     op1=ALU.mult,
@@ -260,5 +264,7 @@ def tile_stulayer_pa_t_kernel(tc, src, ln1_w, ln1_b, w_uvqk, b_uvqk, out):
             if live(quantising):
                 quantise(quantising)
                 project(quantising)
+            if live(fresh):
+                prepare(fresh)
             if live(leaving):
                 finish(leaving)

@@ -62,12 +62,12 @@ def tile_stulayer_pa_t_kernel(tc, src, ln1_w, ln1_b, w_uvqk, b_uvqk, out):
             x.append(keep.tile([P, WIDTHS[u], D], BF16, name="x%d" % u))
         w_planes = keep.tile([P, PASSES, PACK, N], BF16)
         bias = keep.tile([P, N], BF16)
+        w_halves = w_uvqk.rearrange("(g p t) n -> g p t n", t=PACK, p=P)
         for u in range(UNITS):
             nc.sync.dma_start(out=x[u][:], in_=rows_of(src_rows, u))
-            if u == 1:
-                nc.sync.dma_start(
-                    out=w_planes[:], in_=w_uvqk.rearrange("(g p t) n -> p g t n", t=PACK, p=P)
-                )
+            if u in (0, 2):
+                g = u // 2
+                nc.sync.dma_start(out=w_planes[:, g], in_=w_halves[g])
             if u == 5:
                 nc.sync.dma_start(out=bias[:], in_=b_uvqk.partition_broadcast(P))
 
@@ -89,7 +89,7 @@ def tile_stulayer_pa_t_kernel(tc, src, ln1_w, ln1_b, w_uvqk, b_uvqk, out):
         w_grouped = keep.tile([P, PASSES, N, PACK], BF16, align_bytes=64)
         w_codes = keep.tile([P, PASSES, N], U32, align_bytes=64)
         w_scales = keep.tile([P, PASSES, N], U8, align_bytes=64)
-        for g in range(PASSES):
+        def group_weights(g):
             side_by_side(nc.scalar.copy, w_grouped[:, g], w_planes[:, g])
 
         def quantise_weights():
@@ -99,6 +99,7 @@ def tile_stulayer_pa_t_kernel(tc, src, ln1_w, ln1_b, w_uvqk, b_uvqk, out):
                 in_=w_grouped[:].rearrange("p g n t -> p (g n t)"),
             )
 
+        parts_of = {}
         mean_var = {}
         var_eps = {}
         neg_mean = {}
@@ -118,9 +119,12 @@ def tile_stulayer_pa_t_kernel(tc, src, ln1_w, ln1_b, w_uvqk, b_uvqk, out):
                     nc.vector.bn_stats(
                         out=parts[:, j, b, :], in_=x[u][:, j, b * BN_WIDTH : (b + 1) * BN_WIDTH]
                     )
-            for j in range(n):
+            parts_of[u] = parts
+
+        def aggregate(u):
+            for j in range(WIDTHS[u]):
                 nc.vector.bn_aggr(
-                    out=mean_var[u][:, j, :], in_=parts[:, j].rearrange("p b s -> p (b s)")
+                    out=mean_var[u][:, j, :], in_=parts_of[u][:, j].rearrange("p b s -> p (b s)")
                 )
 
         def prepare(u):
@@ -247,24 +251,28 @@ def tile_stulayer_pa_t_kernel(tc, src, ln1_w, ln1_b, w_uvqk, b_uvqk, out):
                     group(u - 1, 1)
             group(u, 0)
 
+        group_weights(0)
         for step in range(UNITS + DEPTH):
             fresh, ready, turning, turned, quantising, leaving = (step - d for d in range(DEPTH + 1))
+            if live(fresh):
+                statistics(fresh)
+                aggregate(fresh)
             if live(turned):
                 scale(turned, [VECTOR_CHUNK], True)
             if live(fresh):
-                statistics(fresh)
-            if step == 3:
-                quantise_weights()
+                prepare(fresh)
             if live(ready):
                 normalise(ready)
             if live(turning):
                 turn_and_scale(turning)
             elif turned == UNITS - 1:
                 group(turned, 1)
+            if step == 3:
+                group_weights(1)
+            if step == 4:
+                quantise_weights()
             if live(quantising):
                 quantise(quantising)
                 project(quantising)
-            if live(fresh):
-                prepare(fresh)
             if live(leaving):
                 finish(leaving)

@@ -26,7 +26,7 @@ UNITS = len(WIDTHS)
 WIDEST = max(WIDTHS)
 FIRST_TILE = [sum(WIDTHS[:u]) for u in range(UNITS)]
 DEPTH = 5
-VECTOR_CHUNK = CHUNKS - 1
+LATE = UNITS - 3
 
 FLOPS = 2 * ROWS * D * N
 
@@ -109,6 +109,7 @@ def tile_stulayer_pa_t_kernel(tc, src, ln1_w, ln1_b, w_uvqk, b_uvqk, out):
         grouped_of = {}
         codes_of = {}
         sums_of = {}
+        result_of = {}
 
         def statistics(u):
             n = WIDTHS[u]
@@ -145,15 +146,17 @@ def tile_stulayer_pa_t_kernel(tc, src, ln1_w, ln1_b, w_uvqk, b_uvqk, out):
                 out=rstd[:], in0=var_eps[u][:], in1=minus_half[:, 0:n], op=ALU.pow
             )
             y = work.tile([P, n, D], F32)
+            span = K_PASS if u == 0 else D
             for j in range(n):
-                nc.gpsimd.tensor_scalar(
-                    out=y[:, j, :].rearrange("p (g t q) -> p g t q", g=PASSES, t=PACK),
-                    in0=x[u][:, j, :].rearrange("p (g q t) -> p g t q", g=PASSES, t=PACK),
-                    scalar1=neg_mean[u][:, j : j + 1],
-                    scalar2=rstd[:, j : j + 1],
-                    op0=ALU.add,
-                    op1=ALU.mult,
-                )
+                for k in range(0, D, span):
+                    nc.gpsimd.tensor_scalar(
+                        out=y[:, j, k : k + span].rearrange("p (g t q) -> p g t q", t=PACK, q=P),
+                        in0=x[u][:, j, k : k + span].rearrange("p (g q t) -> p g t q", t=PACK, q=P),
+                        scalar1=neg_mean[u][:, j : j + 1],
+                        scalar2=rstd[:, j : j + 1],
+                        op0=ALU.add,
+                        op1=ALU.mult,
+                    )
             normed[u] = y
 
         def turn(u, g):
@@ -166,7 +169,7 @@ def tile_stulayer_pa_t_kernel(tc, src, ln1_w, ln1_b, w_uvqk, b_uvqk, out):
                 )
             per_bank = BANK_F32 // (n * P)
             for c in chunks_of(g):
-                if c == VECTOR_CHUNK:
+                if c in vector_chunks(u):
                     bank, slot = vector_pool.tile([P, per_bank, n * P], F32, name="for_vector"), 0
                 else:
                     slot = c % per_bank
@@ -178,6 +181,9 @@ def tile_stulayer_pa_t_kernel(tc, src, ln1_w, ln1_b, w_uvqk, b_uvqk, out):
                     nc.tensor.transpose(
                         bank[:, slot, j * P : (j + 1) * P], y[:, j, c * P : (c + 1) * P], ident[:]
                     )
+
+        def vector_chunks(u):
+            return [] if u >= LATE else [CHUNKS - 1]
 
         def chunks_of(g):
             return range(g * PACK, (g + 1) * PACK)
@@ -197,9 +203,9 @@ def tile_stulayer_pa_t_kernel(tc, src, ln1_w, ln1_b, w_uvqk, b_uvqk, out):
                         out=into, in_=chunk, func=ACT.Identity, scale=gain, bias=shift
                     )
 
-        def group(u, g):
+        def group(copy, u, g):
             side_by_side(
-                nc.scalar.copy, grouped_of[u][:, g], planes_of[u][:, g * PACK : (g + 1) * PACK, :]
+                copy, grouped_of[u][:, g], planes_of[u][:, g * PACK : (g + 1) * PACK, :]
             )
 
         def quantise(u):
@@ -231,14 +237,16 @@ def tile_stulayer_pa_t_kernel(tc, src, ln1_w, ln1_b, w_uvqk, b_uvqk, out):
                     )
                 sums_of[u].append(sums)
 
-        def finish(u):
+        def finish(u, tiles):
             n = WIDTHS[u]
-            result = work.tile([P, n, N], F32)
-            for j in range(n):
+            for j in tiles:
+                if j == 0:
+                    result_of[u] = work.tile([P, n, N], F32, name="result")
                 nc.vector.tensor_tensor(
-                    out=result[:, j, :], in0=sums_of[u][j][:], in1=bias[:], op=ALU.add
+                    out=result_of[u][:, j, :], in0=sums_of[u][j][:], in1=bias[:], op=ALU.add
                 )
-            nc.sync.dma_start(out=rows_of(out_rows, u), in_=result[:])
+                if j == n - 1:
+                    nc.sync.dma_start(out=rows_of(out_rows, u), in_=result_of[u][:])
 
         def live(u):
             return 0 <= u < UNITS
@@ -246,27 +254,28 @@ def tile_stulayer_pa_t_kernel(tc, src, ln1_w, ln1_b, w_uvqk, b_uvqk, out):
         def turn_and_scale(u):
             for g in range(PASSES):
                 turn(u, g)
-                scale(u, [c for c in chunks_of(g) if c != VECTOR_CHUNK], False)
-                if g == 0 and u > 0:
-                    group(u - 1, 1)
-            group(u, 0)
+                scale(u, [c for c in chunks_of(g) if c not in vector_chunks(u)], False)
+                if g == 0 and 0 < u <= LATE:
+                    group(nc.scalar.copy, u - 1, 1)
+            if u < LATE:
+                group(nc.scalar.copy, u, 0)
 
         group_weights(0)
         for step in range(UNITS + DEPTH):
             fresh, ready, turning, turned, quantising, leaving = (step - d for d in range(DEPTH + 1))
             if live(fresh):
                 statistics(fresh)
-                aggregate(fresh)
             if live(turned):
-                scale(turned, [VECTOR_CHUNK], True)
+                scale(turned, vector_chunks(turned), True)
             if live(fresh):
+                aggregate(fresh)
+                if live(leaving):
+                    finish(leaving, [0])
                 prepare(fresh)
             if live(ready):
                 normalise(ready)
             if live(turning):
                 turn_and_scale(turning)
-            elif turned == UNITS - 1:
-                group(turned, 1)
             if step == 3:
                 group_weights(1)
             if step == 4:
@@ -274,5 +283,8 @@ def tile_stulayer_pa_t_kernel(tc, src, ln1_w, ln1_b, w_uvqk, b_uvqk, out):
             if live(quantising):
                 quantise(quantising)
                 project(quantising)
+            if LATE <= turned < UNITS:
+                for g in range(PASSES):
+                    group(nc.vector.tensor_copy, turned, g)
             if live(leaving):
-                finish(leaving)
+                finish(leaving, range(1 if live(fresh) else 0, WIDTHS[leaving]))

import concourse.mybir as mybir
from concourse.masks import make_identity

F32 = mybir.dt.float32
BF16 = mybir.dt.bfloat16
U32 = mybir.dt.uint32
U8 = mybir.dt.uint8
FP8X4 = mybir.dt.float8_e4m3fn_x4
ALU = mybir.AluOpType
ACT = mybir.ActivationFunctionType

P = 128
ROWS = 2048 * 2
D = 1024
N = 512
EPS = 1e-5
PACK = 4
K_PASS = P * PACK
PASSES = D // K_PASS
CHUNKS = D // P
BN_WIDTH = 512
BN_PARTS = D // BN_WIDTH
BANK_F32 = 512
WIDTHS = [1, 1] + [2] * 14 + [1, 1]
UNITS = len(WIDTHS)
WIDEST = max(WIDTHS)
FIRST_TILE = [sum(WIDTHS[:u]) for u in range(UNITS)]
DEPTH = 5
LATE = UNITS - 3

FLOPS = 2 * ROWS * D * N


def side_by_side(copy, grouped, planes):
    copy(
        out=grouped.rearrange("p (c i) t -> p c t i", i=4),
        in_=planes.rearrange("p t (c i) -> p c t i", i=4),
    )


def tile_stulayer_pa_t_kernel(tc, src, ln1_w, ln1_b, w_uvqk, b_uvqk, out):
    nc = tc.nc
    src_rows = src.flatten_outer_dims()
    out_rows = out.flatten_outer_dims()

    def rows_of(tensor, u):
        n = WIDTHS[u]
        first = FIRST_TILE[u] * P
        return tensor[first : first + n * P, :].rearrange("(p j) d -> p j d", j=n)

    with (
        tc.tile_pool(name="keep", bufs=1) as keep,
        tc.tile_pool(name="stat", bufs=4) as stat,
        tc.tile_pool(name="work", bufs=3) as work,
        tc.psum_pool(name="turned", bufs=4) as turned_pool,
        tc.psum_pool(name="vector", bufs=1) as vector_pool,
        tc.psum_pool(name="sums", bufs=3) as sums_pool,
        tc.manual_schedule(),
    ):
        x = []
        for u in range(UNITS):
            x.append(keep.tile([P, WIDTHS[u], D], BF16, name="x%d" % u))
        w_planes = keep.tile([P, PASSES, PACK, N], BF16)
        bias = keep.tile([P, N], BF16)
        w_halves = w_uvqk.rearrange("(g p t) n -> g p t n", t=PACK, p=P)
        for u in range(UNITS):
            nc.sync.dma_start(out=x[u][:], in_=rows_of(src_rows, u))
            if u in (0, 2):
                g = u // 2
                nc.sync.dma_start(out=w_planes[:, g], in_=w_halves[g])
            if u == 5:
                nc.sync.dma_start(out=bias[:], in_=b_uvqk.partition_broadcast(P))

        gain_bf16 = keep.tile([P, PASSES, PACK], BF16)
        shift_bf16 = keep.tile([P, PASSES, PACK], BF16)
        nc.scalar.dma_start(out=gain_bf16[:], in_=ln1_w.rearrange("(g p t) -> p g t", t=PACK, p=P))
        nc.scalar.dma_start(out=shift_bf16[:], in_=ln1_b.rearrange("(g p t) -> p g t", t=PACK, p=P))

        ident = keep.tile([P, P], F32)
        make_identity(nc, ident[:])
        minus_half = keep.tile([P, WIDEST], F32)
        nc.vector.memset(minus_half[:], -0.5)
        gain_shift = keep.tile([P, 2 * CHUNKS], F32)
        nc.scalar.copy(out=gain_shift[:, 0:CHUNKS], in_=gain_bf16[:].rearrange("p g t -> p (g t)"))
        nc.scalar.copy(
            out=gain_shift[:, CHUNKS : 2 * CHUNKS], in_=shift_bf16[:].rearrange("p g t -> p (g t)")
        )

        w_grouped = keep.tile([P, PASSES, N, PACK], BF16, align_bytes=64)
        w_codes = keep.tile([P, PASSES, N], U32, align_bytes=64)
        w_scales = keep.tile([P, PASSES, N], U8, align_bytes=64)
        def group_weights(g):
            side_by_side(nc.scalar.copy, w_grouped[:, g], w_planes[:, g])

        def quantise_weights():
            nc.vector.quantize_mx(
                out=w_codes[:].rearrange("p g n -> p (g n)").bitcast(FP8X4),
                scales=w_scales[:].rearrange("p g n -> p (g n)"),
                in_=w_grouped[:].rearrange("p g n t -> p (g n t)"),
            )

        parts_of = {}
        mean_var = {}
        var_eps = {}
        neg_mean = {}
        normed = {}
        turned_of = {}
        planes_of = {}
        grouped_of = {}
        codes_of = {}
        sums_of = {}
        result_of = {}

        def statistics(u):
            n = WIDTHS[u]
            parts = stat.tile([P, n, BN_PARTS, 6], F32, name="parts")
            mean_var[u] = stat.tile([P, n, 2], F32, name="mv")
            for j in range(n):
                for b in range(BN_PARTS):
                    nc.vector.bn_stats(
                        out=parts[:, j, b, :], in_=x[u][:, j, b * BN_WIDTH : (b + 1) * BN_WIDTH]
                    )
            parts_of[u] = parts

        def aggregate(u):
            for j in range(WIDTHS[u]):
                nc.vector.bn_aggr(
                    out=mean_var[u][:, j, :], in_=parts_of[u][:, j].rearrange("p b s -> p (b s)")
                )

        def prepare(u):
            n = WIDTHS[u]
            var_eps[u] = stat.tile([P, n], F32, name="var_eps")
            nc.vector.tensor_scalar(
                out=var_eps[u][:], in0=mean_var[u][:, :, 1], scalar1=EPS, scalar2=None, op0=ALU.add
            )
            neg_mean[u] = stat.tile([P, n], F32, name="neg_mean")
            nc.vector.tensor_scalar(
                out=neg_mean[u][:], in0=mean_var[u][:, :, 0], scalar1=-1.0, scalar2=None, op0=ALU.mult
            )

        def normalise(u):
            n = WIDTHS[u]
            rstd = stat.tile([P, n], F32)
            nc.gpsimd.tensor_tensor(
                out=rstd[:], in0=var_eps[u][:], in1=minus_half[:, 0:n], op=ALU.pow
            )
            y = work.tile([P, n, D], F32)
            span = K_PASS if u == 0 else D
            for j in range(n):
                for k in range(0, D, span):
                    nc.gpsimd.tensor_scalar(
                        out=y[:, j, k : k + span].rearrange("p (g t q) -> p g t q", t=PACK, q=P),
                        in0=x[u][:, j, k : k + span].rearrange("p (g q t) -> p g t q", t=PACK, q=P),
                        scalar1=neg_mean[u][:, j : j + 1],
                        scalar2=rstd[:, j : j + 1],
                        op0=ALU.add,
                        op1=ALU.mult,
                    )
            normed[u] = y

        def turn(u, g):
            n = WIDTHS[u]
            y = normed[u]
            if g == 0:
                planes_of[u] = work.tile([P, CHUNKS, n * P], BF16, name="planes")
                grouped_of[u] = work.tile(
                    [P, PASSES, n * P, PACK], BF16, align_bytes=64, name="grouped"
                )
            per_bank = BANK_F32 // (n * P)
            for c in chunks_of(g):
                if c in vector_chunks(u):
                    bank, slot = vector_pool.tile([P, per_bank, n * P], F32, name="for_vector"), 0
                else:
                    slot = c % per_bank
                    if slot == 0:
                        shared = turned_pool.tile([P, per_bank, n * P], F32, name="turned")
                    bank = shared
                turned_of[u, c] = bank[:, slot, :]
                for j in range(n):
                    nc.tensor.transpose(
                        bank[:, slot, j * P : (j + 1) * P], y[:, j, c * P : (c + 1) * P], ident[:]
                    )

        def vector_chunks(u):
            return [] if u >= LATE else [CHUNKS - 1]

        def chunks_of(g):
            return range(g * PACK, (g + 1) * PACK)

        def scale(u, chunks, on_vector):
            for c in chunks:
                gain = gain_shift[:, c : c + 1]
                shift = gain_shift[:, CHUNKS + c : CHUNKS + c + 1]
                into = planes_of[u][:, c, :]
                chunk = turned_of[u, c]
                if on_vector:
                    nc.vector.tensor_scalar(
                        out=into, in0=chunk, scalar1=gain, scalar2=shift, op0=ALU.mult, op1=ALU.add
                    )
                else:
                    nc.scalar.activation(
                        out=into, in_=chunk, func=ACT.Identity, scale=gain, bias=shift
                    )

        def group(copy, u, g):
            side_by_side(
                copy, grouped_of[u][:, g], planes_of[u][:, g * PACK : (g + 1) * PACK, :]
            )

        def quantise(u):
            n = WIDTHS[u]
            codes = work.tile([P, PASSES, n * P], U32, align_bytes=64)
            scales = work.tile([P, PASSES, n * P], U8, align_bytes=64)
            nc.vector.quantize_mx(
                out=codes[:].rearrange("p g c -> p (g c)").bitcast(FP8X4),
                scales=scales[:].rearrange("p g c -> p (g c)"),
                in_=grouped_of[u][:].rearrange("p g c t -> p (g c t)"),
            )
            codes_of[u] = (codes, scales)

        def project(u):
            codes, scales = codes_of[u]
            sums_of[u] = []
            for j in range(WIDTHS[u]):
                rows = slice(j * P, (j + 1) * P)
                sums = sums_pool.tile([P, N], F32)
                for g in range(PASSES):
                    nc.tensor.matmul_mx(
                        out=sums[:],
                        lhsT=codes[:, g, rows].bitcast(FP8X4),
                        lhsT_scale=scales[:, g, rows],
                        rhs=w_codes[:, g, :].bitcast(FP8X4),
                        rhs_scale=w_scales[:, g, :],
                        start=(g == 0),
                        stop=(g == PASSES - 1),
                    )
                sums_of[u].append(sums)

        def finish(u, tiles):
            n = WIDTHS[u]
            for j in tiles:
                if j == 0:
                    result_of[u] = work.tile([P, n, N], F32, name="result")
                nc.vector.tensor_tensor(
                    out=result_of[u][:, j, :], in0=sums_of[u][j][:], in1=bias[:], op=ALU.add
                )
                if j == n - 1:
                    nc.sync.dma_start(out=rows_of(out_rows, u), in_=result_of[u][:])

        def live(u):
            return 0 <= u < UNITS

        def turn_and_scale(u):
            for g in range(PASSES):
                turn(u, g)
                scale(u, [c for c in chunks_of(g) if c not in vector_chunks(u)], False)
                if g == 0 and 0 < u <= LATE:
                    group(nc.scalar.copy, u - 1, 1)
            if u < LATE:
                group(nc.scalar.copy, u, 0)

        group_weights(0)
        for step in range(UNITS + DEPTH):
            fresh, ready, turning, turned, quantising, leaving = (step - d for d in range(DEPTH + 1))
            if live(fresh):
                statistics(fresh)
            if live(turned):
                scale(turned, vector_chunks(turned), True)
            if live(fresh):
                aggregate(fresh)
                if live(leaving):
                    finish(leaving, [0])
                prepare(fresh)
            if live(ready):
                normalise(ready)
            if live(turning):
                turn_and_scale(turning)
            if step == 3:
                group_weights(1)
            if step == 4:
                quantise_weights()
            if live(quantising):
                quantise(quantising)
                project(quantising)
            if LATE <= turned < UNITS:
                for g in range(PASSES):
                    group(nc.vector.tensor_copy, turned, g)
            if live(leaving):
                finish(leaving, range(1 if live(fresh) else 0, WIDTHS[leaving]))
